import numpy as np
import ml_dtypes


def mxq(x, axis, fmt="e4m3"):
    dtype, down = {"e4m3": (ml_dtypes.float8_e4m3fn, 7), "e5m2": (ml_dtypes.float8_e5m2, 14)}[fmt]
    v = np.moveaxis(np.asarray(x, np.float32).astype(ml_dtypes.bfloat16).astype(np.float64), axis, -1)
    blocks = v.reshape(v.shape[:-1] + (-1, 32))
    amax = np.abs(blocks).max(-1, keepdims=True)
    byte = np.maximum(np.where(amax > 0, np.frexp(amax)[1] - 1 + 127, 0) - down, 1)
    scale = np.exp2(byte - 127.0)
    codes = (blocks / scale).astype(np.float32).astype(dtype).astype(np.float64)
    return np.moveaxis((codes * scale).reshape(v.shape), -1, axis)


WIDE = False


def mx_kscale(k):
    if not WIDE:
        return np.ones(k)
    levels = np.array([10, -10, 5, -5, 0])
    if k % 512:
        return np.exp2(np.random.permutation(np.resize(levels, k // 32))).repeat(32)
    a = np.empty((k // 512, 16))
    for p in range(k // 512):
        a[p, :8] = np.random.permutation(np.resize(levels, 8))
        for g in range(8):
            far = levels[np.abs(levels - a[p, g]) >= 10]
            a[p, g + 8] = far[np.random.randint(len(far))]
    return np.exp2(a.ravel()).repeat(32)


BF16 = ml_dtypes.bfloat16


def bf(x):
    return np.asarray(x, np.float32).astype(BF16)


def f64(x):
    return np.asarray(x).astype(np.float64)


B, S, HID, NH, DH = 4, 256, 1024, 16, 64
DQ = NH * DH


def setup_inputs():
    s = mx_kscale(DQ)
    y = np.random.standard_normal((B, S, DQ)) * 0.3 * s
    h = np.ascontiguousarray(y.reshape(B, NH, S, DH).transpose(0, 2, 1, 3))
    return {"h_attn": bf(h),
            "Wo": bf(np.random.standard_normal((DQ, HID)) * 1.5 / np.sqrt(DQ) / s[:, None]),
            "bo": bf(np.random.standard_normal(HID) * 0.3)}


def core(h_attn, Wo, bo):
    y = f64(h_attn).transpose(0, 2, 1, 3).reshape(B, -1, DQ)
    return (mxq(y, 2, "e4m3") @ mxq(f64(Wo), 0, "e4m3")) + f64(bo)


def e4m3fn_bytes(y):
    return np.clip(np.asarray(y, np.float64), -448.0, 448.0).astype(np.float32).astype(ml_dtypes.float8_e4m3fn).view(np.uint8)


Y_SCALE = 400.0


def reference(h_attn, Wo, bo):
    out = core(h_attn, Wo, bo)
    return out, e4m3fn_bytes(out * Y_SCALE)

@@ -1,0 +1,202 @@
+from contextlib import ExitStack
+
+import concourse.mybir as mybir
+from concourse.masks import make_identity
+
+FLOPS = 2 * 1024 * 1024 * 1024
+
+F32 = mybir.dt.float32
+BF16 = mybir.dt.bfloat16
+U32 = mybir.dt.uint32
+U8 = mybir.dt.uint8
+FP8X4 = mybir.dt.float8_e4m3fn_x4
+FP8 = mybir.dt.float8_e4m3fn
+ADD = mybir.AluOpType.add
+MULT = mybir.AluOpType.mult
+COPY = mybir.ActivationFunctionType.Copy
+
+P = 128
+Y_SCALE = 400.0
+
+W_MODE = {(0, 0): "vv", (0, 1): "pp", (1, 0): "vp", (1, 1): "pp"}
+V_CASTS = ((1, 3, 1),)
+
+
+def tile_reasoningmultiheadattention_pb_kernel(tc, h_attn, Wo, bo, out_0, out_1):
+    nc = tc.nc
+    with ExitStack() as ctx:
+        keep = ctx.enter_context(tc.tile_pool(name="keep", bufs=1))
+        tps = ctx.enter_context(tc.psum_pool(name="tps", bufs=3))
+        accs = ctx.enter_context(tc.psum_pool(name="accs", bufs=5))
+
+        yv = h_attn.rearrange("b (x j) h d -> (b x) j (h d)", j=8)
+        wv = Wo.rearrange("(g p t) n -> g p t n", g=2, t=4)
+
+        T = [keep.tile([P, 8, 512], BF16, name="T%d" % hh) for hh in range(2)]
+        R = [keep.tile([P, 8, 8, 64], BF16, name="R%d" % hh, align_bytes=64) for hh in range(2)]
+        G = [keep.tile([P, 8, 128, 2], F32, name="G%d" % hh, align_bytes=64) for hh in range(2)]
+        a_codes = [keep.tile([P, 1024], U32, name="ac%d" % hh, align_bytes=64) for hh in range(2)]
+        a_scales = [keep.tile([P, 1024], U8, name="as%d" % hh, align_bytes=64) for hh in range(2)]
+        Wraw = {}
+        Wg = {}
+        for nh in range(2):
+            for g in range(2):
+                Wraw[(nh, g)] = keep.tile([P, 4, 512], BF16, name="wr%d%d" % (nh, g))
+                Wg[(nh, g)] = keep.tile([P, 512, 4], BF16, name="wg%d%d" % (nh, g), align_bytes=64)
+        b_codes = [keep.tile([P, 1024], U32, name="bc%d" % g, align_bytes=64) for g in range(2)]
+        b_scales = [keep.tile([P, 1024], U8, name="bs%d" % g, align_bytes=64) for g in range(2)]
+        o0 = {}
+        o1 = {}
+        for hh in range(2):
+            for b in range(4):
+                o0[(hh, b)] = keep.tile([P, 1024], F32, name="o0_%d%d" % (hh, b))
+                o1[(hh, b)] = keep.tile([P, 1024], FP8, name="o1_%d%d" % (hh, b))
+
+        ident = keep.tile([P, P], F32, name="ident")
+        perm = keep.tile([P, P], F32, name="perm")
+        ones = keep.tile([P, P], BF16, name="ones")
+        identb = keep.tile([P, P], BF16, name="identb")
+        brow = keep.tile([P, 1024], BF16, name="brow")
+        bias = keep.tile([P, 1024], F32, name="bias")
+
+        def load_y(hh, jh):
+            nc.sync.dma_start(
+                out=T[hh][:, 4 * jh : 4 * jh + 4, :],
+                in_=yv[:, 4 * jh : 4 * jh + 4, 512 * hh : 512 * hh + 512],
+            )
+
+        def load_w(nh, g):
+            nc.sync.dma_start(out=Wraw[(nh, g)][:], in_=wv[g][:, :, 512 * nh : 512 * nh + 512])
+
+        nc.vector.memset(brow[:], 0.0)
+        nc.sync.dma_start(out=brow[0:1, :], in_=bo.rearrange("(o n) -> o n", o=1))
+        load_y(0, 0)
+        load_y(0, 1)
+        load_w(0, 0)
+        load_w(0, 1)
+        load_y(1, 0)
+        load_y(1, 1)
+        load_w(1, 0)
+        load_w(1, 1)
+
+        make_identity(nc, ident[:])
+        nc.gpsimd.memset(ones[:], 1.0)
+        make_identity(nc, identb[:])
+        nc.vector.tensor_copy(
+            out=perm[:].rearrange("p (g b q) -> p g b q", g=2, b=4),
+            in_=ident[:].rearrange("p (b q g) -> p g b q", b=4, g=2),
+        )
+        for nh in range(2):
+            ps = accs.tile([P, 512], F32, name="acc")
+            nc.tensor.matmul(out=ps[:], lhsT=ones[:], rhs=brow[:, 512 * nh : 512 * nh + 512], start=True, stop=True)
+            nc.scalar.copy(out=bias[:, 512 * nh : 512 * nh + 512], in_=ps[:])
+
+        def relayout(hh, jh):
+            nc.vector.tensor_copy(
+                out=R[hh][:, :, 4 * jh : 4 * jh + 4, :],
+                in_=T[hh][:, 4 * jh : 4 * jh + 4, :].rearrange("p j (h d) -> p h j d", d=64),
+            )
+
+        def turn(hh, hp):
+            rw = R[hh][:].rearrange("p h j d -> p (h j d)").bitcast(F32)
+            pt = tps.tile([P, 2, 8, 2, 16], F32, name="pt", tag="tp")
+            for hl in range(2):
+                for u in range(2):
+                    h = 2 * hp + hl
+                    nc.tensor.transpose(out=pt[:, u, :, hl, :], in_=rw[:, 256 * h + u : 256 * (h + 1) : 2], identity=perm[:])
+            nc.scalar.copy(
+                out=G[hh][:, :, 32 * hp : 32 * hp + 32, :],
+                in_=pt[:].rearrange("p u a hl q -> p a (hl q) u"),
+            )
+
+        def yquant(hh, g):
+            gb = G[hh][:].rearrange("p a m u -> p (a m u)").bitcast(BF16)
+            nc.vector.quantize_mx(
+                out=a_codes[hh][:, 512 * g : 512 * g + 512].bitcast(FP8X4),
+                scales=a_scales[hh][:, 512 * g : 512 * g + 512],
+                in_=gb[:, 2048 * g : 2048 * g + 2048],
+            )
+
+        def winter(nh, g):
+            src = Wraw[(nh, g)][:].rearrange("p t c -> p c t")
+            if W_MODE[(nh, g)] == "vv":
+                nc.vector.tensor_copy(out=Wg[(nh, g)][:], in_=src)
+                return
+            for k in range(2):
+                if W_MODE[(nh, g)][k] == "v":
+                    nc.vector.tensor_copy(
+                        out=Wg[(nh, g)][:, 256 * k : 256 * k + 256, :], in_=src[:, 256 * k : 256 * k + 256, :]
+                    )
+                else:
+                    pw = tps.tile([P, 256, 4], BF16, name="pw", tag="tp")
+                    for s in range(2):
+                        c0 = 256 * k + 128 * s
+                        nc.tensor.matmul(
+                            out=pw[:, 128 * s : 128 * s + 128, :],
+                            lhsT=identb[:],
+                            rhs=src[:, c0 : c0 + 128, :],
+                            start=True,
+                            stop=True,
+                        )
+                    nc.scalar.copy(out=Wg[(nh, g)][:, 256 * k : 256 * k + 256, :], in_=pw[:])
+
+        def wquant(nh, g):
+            nc.vector.quantize_mx(
+                out=b_codes[g][:, 512 * nh : 512 * nh + 512].bitcast(FP8X4),
+                scales=b_scales[g][:, 512 * nh : 512 * nh + 512],
+                in_=Wg[(nh, g)][:].rearrange("p c t -> p (c t)"),
+            )
+
+        def mx(hh, b, nh):
+            cols = slice(512 * nh, 512 * nh + 512)
+            acc = accs.tile([P, 512], F32, name="acc")
+            for g in range(2):
+                a = 4 * g + b
+                nc.tensor.matmul_mx(
+                    out=acc[:],
+                    lhsT=a_codes[hh][:, 128 * a : 128 * a + 128].bitcast(FP8X4),
+                    lhsT_scale=a_scales[hh][:, 128 * a : 128 * a + 128],
+                    rhs=b_codes[g][:, cols].bitcast(FP8X4),
+                    rhs_scale=b_scales[g][:, cols],
+                    start=(g == 0),
+                    stop=(g == 1),
+                )
+            res = o0[(hh, b)]
+            byt = o1[(hh, b)]
+            nc.vector.tensor_tensor(out=res[:, cols], in0=acc[:], in1=bias[:, cols], op=ADD)
+            nc.sync.dma_start(out=out_0[b, 128 * hh : 128 * hh + 128, cols], in_=res[:, cols])
+            if (hh, b, nh) in V_CASTS:
+                nc.vector.tensor_scalar(
+                    out=byt[:, cols], in0=res[:, cols], scalar1=Y_SCALE, scalar2=None, op0=MULT, saturate=False
+                )
+            else:
+                nc.scalar.activation(out=byt[:, cols], in_=res[:, cols], func=COPY, scale=Y_SCALE, saturate=False)
+            nc.sync.dma_start(out=out_1[b, 128 * hh : 128 * hh + 128, cols], in_=byt[:, cols].bitcast(U8))
+
+        relayout(0, 0)
+        relayout(0, 1)
+        for hp in range(4):
+            turn(0, hp)
+        winter(0, 0)
+        winter(0, 1)
+        wquant(0, 0)
+        yquant(0, 0)
+        yquant(0, 1)
+        wquant(0, 1)
+        for b in range(4):
+            mx(0, b, 0)
+        relayout(1, 0)
+        relayout(1, 1)
+        for hp in range(4):
+            turn(1, hp)
+        yquant(1, 0)
+        yquant(1, 1)
+        for b in range(4):
+            mx(1, b, 0)
+        winter(1, 0)
+        winter(1, 1)
+        wquant(1, 0)
+        wquant(1, 1)
+        for hh in range(2):
+            for b in range(4):
+                mx(hh, b, 1)

@@ -18,8 +18,25 @@ COPY = mybir.ActivationFunctionType.Copy
 P = 128
 Y_SCALE = 400.0
 
-W_MODE = {(0, 0): "vv", (0, 1): "pp", (1, 0): "vp", (1, 1): "pp"}
-V_CASTS = ((1, 3, 1),)
+LOADS = ("y00", "y01", "b", "w00", "w01", "w10", "w11", "y10", "y11")
+V_CASTS = ()
+V_YC = ()
+V_WC = ()
+S_WH = ()
+ORDER = (
+    "bm0", "bm1", "bc0", "bc1", "rl00", "rl01", "tr00", "wv00", "tr01", "yc00",
+    "tr02", "yc01", "tr03", "yc02", "wq00", "wm010", "yc03", "wm011", "wc010", "yq00",
+    "wm101", "wc011", "yq01", "wc101", "wq01", "wm110", "wh100", "wm111", "wc110", "mx000",
+    "wq10", "wc111", "mx010", "rl10", "mx020", "wq11", "mx030", "rl11", "mx001", "ad000",
+    "tr10", "ad010", "ca000", "tr11", "ad020", "yc10", "tr12", "s0000", "ad030", "mx011",
+    "yc11", "s0010", "ad001", "yc12", "tr13", "s0020", "ad011", "ca010", "mx021", "s0030",
+    "yc13", "s0001", "mx031", "ad021", "ca020", "s0011", "yq10", "ca030", "yq11", "s0021",
+    "ca001", "ad031", "mx100", "ca011", "mx110", "ca021", "ad100", "s100", "mx120", "ca031",
+    "s0031", "ad110", "mx130", "ca100", "s101", "ad120", "s102", "mx101", "ca110", "ad130",
+    "s0100", "mx111", "ca120", "ad101", "s103", "mx121", "s0110", "ca130", "ad111", "mx131",
+    "s0120", "ca101", "ad121", "s0130", "ca111", "ad131", "ca121", "s0101", "ca131", "s0111",
+    "s110", "s0121", "s111", "s0131", "s112", "s113",
+)
 
 
 def tile_reasoningmultiheadattention_pb_kernel(tc, h_attn, Wo, bo, out_0, out_1):
@@ -28,6 +45,7 @@ def tile_reasoningmultiheadattention_pb_kernel(tc, h_attn, Wo, bo, out_0, out_1)
         keep = ctx.enter_context(tc.tile_pool(name="keep", bufs=1))
         tps = ctx.enter_context(tc.psum_pool(name="tps", bufs=3))
         accs = ctx.enter_context(tc.psum_pool(name="accs", bufs=5))
+        ctx.enter_context(tc.manual_schedule())
 
         yv = h_attn.rearrange("b (x j) h d -> (b x) j (h d)", j=8)
         wv = Wo.rearrange("(g p t) n -> g p t n", g=2, t=4)
@@ -58,58 +76,61 @@ def tile_reasoningmultiheadattention_pb_kernel(tc, h_attn, Wo, bo, out_0, out_1)
         identb = keep.tile([P, P], BF16, name="identb")
         brow = keep.tile([P, 1024], BF16, name="brow")
         bias = keep.tile([P, 1024], F32, name="bias")
-
-        def load_y(hh, jh):
-            nc.sync.dma_start(
-                out=T[hh][:, 4 * jh : 4 * jh + 4, :],
-                in_=yv[:, 4 * jh : 4 * jh + 4, 512 * hh : 512 * hh + 512],
-            )
-
-        def load_w(nh, g):
-            nc.sync.dma_start(out=Wraw[(nh, g)][:], in_=wv[g][:, :, 512 * nh : 512 * nh + 512])
+        banks = {}
 
         nc.vector.memset(brow[:], 0.0)
-        nc.sync.dma_start(out=brow[0:1, :], in_=bo.rearrange("(o n) -> o n", o=1))
-        load_y(0, 0)
-        load_y(0, 1)
-        load_w(0, 0)
-        load_w(0, 1)
-        load_y(1, 0)
-        load_y(1, 1)
-        load_w(1, 0)
-        load_w(1, 1)
+        for ld in LOADS:
+            if ld == "b":
+                nc.sync.dma_start(out=brow[0:1, :], in_=bo.rearrange("(o n) -> o n", o=1))
+                continue
+            i = int(ld[1])
+            k = int(ld[2])
+            if ld[0] == "y":
+                nc.sync.dma_start(out=T[i][:, 4 * k : 4 * k + 4, :], in_=yv[:, 4 * k : 4 * k + 4, 512 * i : 512 * i + 512])
+            else:
+                nc.sync.dma_start(out=Wraw[(i, k)][:], in_=wv[k][:, :, 512 * i : 512 * i + 512])
 
-        make_identity(nc, ident[:])
         nc.gpsimd.memset(ones[:], 1.0)
+        make_identity(nc, ident[:])
         make_identity(nc, identb[:])
         nc.vector.tensor_copy(
             out=perm[:].rearrange("p (g b q) -> p g b q", g=2, b=4),
             in_=ident[:].rearrange("p (b q g) -> p g b q", b=4, g=2),
         )
-        for nh in range(2):
-            ps = accs.tile([P, 512], F32, name="acc")
-            nc.tensor.matmul(out=ps[:], lhsT=ones[:], rhs=brow[:, 512 * nh : 512 * nh + 512], start=True, stop=True)
-            nc.scalar.copy(out=bias[:, 512 * nh : 512 * nh + 512], in_=ps[:])
 
-        def relayout(hh, jh):
+        def op_bm(nh):
+            banks[("b", nh)] = accs.tile([P, 512], F32, name="acc")
+            nc.tensor.matmul(
+                out=banks[("b", nh)][:], lhsT=ones[:], rhs=brow[:, 512 * nh : 512 * nh + 512], start=True, stop=True
+            )
+
+        def op_bc(nh):
+            nc.scalar.copy(out=bias[:, 512 * nh : 512 * nh + 512], in_=banks[("b", nh)][:])
+
+        def op_rl(hh, jh):
             nc.vector.tensor_copy(
                 out=R[hh][:, :, 4 * jh : 4 * jh + 4, :],
                 in_=T[hh][:, 4 * jh : 4 * jh + 4, :].rearrange("p j (h d) -> p h j d", d=64),
             )
 
-        def turn(hh, hp):
+        def op_tr(hh, hp):
             rw = R[hh][:].rearrange("p h j d -> p (h j d)").bitcast(F32)
             pt = tps.tile([P, 2, 8, 2, 16], F32, name="pt", tag="tp")
+            banks[("t", hh, hp)] = pt
             for hl in range(2):
                 for u in range(2):
                     h = 2 * hp + hl
                     nc.tensor.transpose(out=pt[:, u, :, hl, :], in_=rw[:, 256 * h + u : 256 * (h + 1) : 2], identity=perm[:])
-            nc.scalar.copy(
-                out=G[hh][:, :, 32 * hp : 32 * hp + 32, :],
-                in_=pt[:].rearrange("p u a hl q -> p a (hl q) u"),
-            )
 
-        def yquant(hh, g):
+        def op_yc(hh, hp):
+            dst = G[hh][:, :, 32 * hp : 32 * hp + 32, :]
+            src = banks[("t", hh, hp)][:].rearrange("p u a hl q -> p a (hl q) u")
+            if "%d%d" % (hh, hp) in V_YC:
+                nc.vector.tensor_copy(out=dst, in_=src)
+            else:
+                nc.scalar.copy(out=dst, in_=src)
+
+        def op_yq(hh, g):
             gb = G[hh][:].rearrange("p a m u -> p (a m u)").bitcast(BF16)
             nc.vector.quantize_mx(
                 out=a_codes[hh][:, 512 * g : 512 * g + 512].bitcast(FP8X4),
@@ -117,39 +138,47 @@ def tile_reasoningmultiheadattention_pb_kernel(tc, h_attn, Wo, bo, out_0, out_1)
                 in_=gb[:, 2048 * g : 2048 * g + 2048],
             )
 
-        def winter(nh, g):
-            src = Wraw[(nh, g)][:].rearrange("p t c -> p c t")
-            if W_MODE[(nh, g)] == "vv":
-                nc.vector.tensor_copy(out=Wg[(nh, g)][:], in_=src)
-                return
-            for k in range(2):
-                if W_MODE[(nh, g)][k] == "v":
-                    nc.vector.tensor_copy(
-                        out=Wg[(nh, g)][:, 256 * k : 256 * k + 256, :], in_=src[:, 256 * k : 256 * k + 256, :]
-                    )
-                else:
-                    pw = tps.tile([P, 256, 4], BF16, name="pw", tag="tp")
-                    for s in range(2):
-                        c0 = 256 * k + 128 * s
-                        nc.tensor.matmul(
-                            out=pw[:, 128 * s : 128 * s + 128, :],
-                            lhsT=identb[:],
-                            rhs=src[:, c0 : c0 + 128, :],
-                            start=True,
-                            stop=True,
-                        )
-                    nc.scalar.copy(out=Wg[(nh, g)][:, 256 * k : 256 * k + 256, :], in_=pw[:])
+        def op_wv(nh, g):
+            nc.vector.tensor_copy(out=Wg[(nh, g)][:], in_=Wraw[(nh, g)][:].rearrange("p t c -> p c t"))
 
-        def wquant(nh, g):
+        def op_ws(nh, g):
+            nc.scalar.copy(out=Wg[(nh, g)][:], in_=Wraw[(nh, g)][:].rearrange("p t c -> p c t"))
+
+        def op_wh(nh, g, k):
+            src = Wraw[(nh, g)][:].rearrange("p t c -> p c t")
+            if "%d%d%d" % (nh, g, k) in S_WH:
+                nc.scalar.copy(out=Wg[(nh, g)][:, 256 * k : 256 * k + 256, :], in_=src[:, 256 * k : 256 * k + 256, :])
+            else:
+                nc.vector.tensor_copy(out=Wg[(nh, g)][:, 256 * k : 256 * k + 256, :], in_=src[:, 256 * k : 256 * k + 256, :])
+
+        def op_wm(nh, g, k):
+            src = Wraw[(nh, g)][:].rearrange("p t c -> p c t")
+            pw = tps.tile([P, 256, 4], BF16, name="pw", tag="tp")
+            banks[("w", nh, g, k)] = pw
+            for s in range(2):
+                c0 = 256 * k + 128 * s
+                nc.tensor.matmul(
+                    out=pw[:, 128 * s : 128 * s + 128, :], lhsT=identb[:], rhs=src[:, c0 : c0 + 128, :], start=True, stop=True
+                )
+
+        def op_wc(nh, g, k):
+            dst = Wg[(nh, g)][:, 256 * k : 256 * k + 256, :]
+            if "%d%d%d" % (nh, g, k) in V_WC:
+                nc.vector.tensor_copy(out=dst, in_=banks[("w", nh, g, k)][:])
+            else:
+                nc.scalar.copy(out=dst, in_=banks[("w", nh, g, k)][:])
+
+        def op_wq(nh, g):
             nc.vector.quantize_mx(
                 out=b_codes[g][:, 512 * nh : 512 * nh + 512].bitcast(FP8X4),
                 scales=b_scales[g][:, 512 * nh : 512 * nh + 512],
                 in_=Wg[(nh, g)][:].rearrange("p c t -> p (c t)"),
             )
 
-        def mx(hh, b, nh):
+        def op_mx(hh, b, nh):
             cols = slice(512 * nh, 512 * nh + 512)
             acc = accs.tile([P, 512], F32, name="acc")
+            banks[("m", hh, b, nh)] = acc
             for g in range(2):
                 a = 4 * g + b
                 nc.tensor.matmul_mx(
@@ -161,42 +190,30 @@ def tile_reasoningmultiheadattention_pb_kernel(tc, h_attn, Wo, bo, out_0, out_1)
                     start=(g == 0),
                     stop=(g == 1),
                 )
-            res = o0[(hh, b)]
-            byt = o1[(hh, b)]
-            nc.vector.tensor_tensor(out=res[:, cols], in0=acc[:], in1=bias[:, cols], op=ADD)
-            nc.sync.dma_start(out=out_0[b, 128 * hh : 128 * hh + 128, cols], in_=res[:, cols])
-            if (hh, b, nh) in V_CASTS:
+
+        def op_ad(hh, b, nh):
+            cols = slice(512 * nh, 512 * nh + 512)
+            nc.vector.tensor_tensor(out=o0[(hh, b)][:, cols], in0=banks[("m", hh, b, nh)][:], in1=bias[:, cols], op=ADD)
+
+        def op_s0(hh, b, nh):
+            cols = slice(512 * nh, 512 * nh + 512)
+            nc.sync.dma_start(out=out_0[b, 128 * hh : 128 * hh + 128, cols], in_=o0[(hh, b)][:, cols])
+
+        def op_ca(hh, b, nh):
+            cols = slice(512 * nh, 512 * nh + 512)
+            if "%d%d%d" % (hh, b, nh) in V_CASTS:
                 nc.vector.tensor_scalar(
-                    out=byt[:, cols], in0=res[:, cols], scalar1=Y_SCALE, scalar2=None, op0=MULT, saturate=False
+                    out=o1[(hh, b)][:, cols], in0=o0[(hh, b)][:, cols], scalar1=Y_SCALE, scalar2=None, op0=MULT, saturate=False
                 )
             else:
-                nc.scalar.activation(out=byt[:, cols], in_=res[:, cols], func=COPY, scale=Y_SCALE, saturate=False)
-            nc.sync.dma_start(out=out_1[b, 128 * hh : 128 * hh + 128, cols], in_=byt[:, cols].bitcast(U8))
+                nc.scalar.activation(out=o1[(hh, b)][:, cols], in_=o0[(hh, b)][:, cols], func=COPY, scale=Y_SCALE, saturate=False)
 
-        relayout(0, 0)
-        relayout(0, 1)
-        for hp in range(4):
-            turn(0, hp)
-        winter(0, 0)
-        winter(0, 1)
-        wquant(0, 0)
-        yquant(0, 0)
-        yquant(0, 1)
-        wquant(0, 1)
-        for b in range(4):
-            mx(0, b, 0)
-        relayout(1, 0)
-        relayout(1, 1)
-        for hp in range(4):
-            turn(1, hp)
-        yquant(1, 0)
-        yquant(1, 1)
-        for b in range(4):
-            mx(1, b, 0)
-        winter(1, 0)
-        winter(1, 1)
-        wquant(1, 0)
-        wquant(1, 1)
-        for hh in range(2):
-            for b in range(4):
-                mx(hh, b, 1)
+        def op_s1(hh, b):
+            nc.sync.dma_start(out=out_1[b, 128 * hh : 128 * hh + 128, :], in_=o1[(hh, b)][:].bitcast(U8))
+
+        table = {
+            "bm": op_bm, "bc": op_bc, "rl": op_rl, "tr": op_tr, "yc": op_yc, "yq": op_yq, "wv": op_wv, "ws": op_ws,
+            "wh": op_wh, "wm": op_wm, "wc": op_wc, "wq": op_wq, "mx": op_mx, "ad": op_ad, "s0": op_s0, "ca": op_ca, "s1": op_s1,
+        }
+        for step in ORDER:
+            table[step[:2]](*[int(c) for c in step[2:]])

@@ -20,22 +20,19 @@ Y_SCALE = 400.0
 
 LOADS = ("y00", "y01", "b", "w00", "w01", "w10", "w11", "y10", "y11")
 V_CASTS = ()
-V_YC = ()
-V_WC = ()
-S_WH = ()
 ORDER = (
-    "bm0", "bm1", "bc0", "bc1", "rl00", "rl01", "tr00", "wv00", "tr01", "yc00",
-    "tr02", "yc01", "tr03", "yc02", "wq00", "wm010", "yc03", "wm011", "wc010", "yq00",
-    "wm101", "wc011", "yq01", "wc101", "wq01", "wm110", "wh100", "wm111", "wc110", "mx000",
-    "wq10", "wc111", "mx010", "rl10", "mx020", "wq11", "mx030", "rl11", "mx001", "ad000",
-    "tr10", "ad010", "ca000", "tr11", "ad020", "yc10", "tr12", "s0000", "ad030", "mx011",
-    "yc11", "s0010", "ad001", "yc12", "tr13", "s0020", "ad011", "ca010", "mx021", "s0030",
-    "yc13", "s0001", "mx031", "ad021", "ca020", "s0011", "yq10", "ca030", "yq11", "s0021",
-    "ca001", "ad031", "mx100", "ca011", "mx110", "ca021", "ad100", "s100", "mx120", "ca031",
-    "s0031", "ad110", "mx130", "ca100", "s101", "ad120", "s102", "mx101", "ca110", "ad130",
-    "s0100", "mx111", "ca120", "ad101", "s103", "mx121", "s0110", "ca130", "ad111", "mx131",
-    "s0120", "ca101", "ad121", "s0130", "ca111", "ad131", "ca121", "s0101", "ca131", "s0111",
-    "s110", "s0121", "s111", "s0131", "s112", "s113",
+    "dm0", "rl00", "rl01", "bm0", "bm1", "bc0", "tr00", "bc1", "tr01", "wv00",
+    "tr02", "yc00", "yc01", "tr03", "yc02", "wv01", "dm1", "yc03", "wq00", "ws10",
+    "dm2", "wq01", "yq00", "dm3", "yq01", "ws11", "wq10", "mx000", "mx010", "rl10",
+    "mx020", "ad000", "mx030", "rl11", "ca000", "ad010", "tr10", "s0000", "tr11", "wq11",
+    "yc10", "tr12", "ad020", "yc11", "s0010", "mx001", "ad030", "yc12", "tr13", "ad001",
+    "ca010", "mx011", "s0020", "yc13", "mx021", "s0030", "ad011", "ca020", "mx031", "s0001",
+    "yq10", "ca030", "yq11", "s0011", "ca001", "ad021", "mx100", "ca011", "ad031", "mx110",
+    "ca021", "s100", "ad100", "mx120", "s0021", "ca031", "mx130", "ad110", "s101", "ca100",
+    "s0031", "mx101", "ad120", "ca110", "mx111", "s102", "ad130", "ca120", "s0100", "mx121",
+    "ad101", "ca130", "s103", "mx131", "ad111", "s0110", "ca101", "ad121", "s0120", "ca111",
+    "ad131", "s0130", "ca121", "s0101", "ca131", "s0111", "s110", "s0121", "s111", "s0131",
+    "s112", "s113",
 )
 
 
@@ -51,7 +48,7 @@ def tile_reasoningmultiheadattention_pb_kernel(tc, h_attn, Wo, bo, out_0, out_1)
         wv = Wo.rearrange("(g p t) n -> g p t n", g=2, t=4)
 
         T = [keep.tile([P, 8, 512], BF16, name="T%d" % hh) for hh in range(2)]
-        R = [keep.tile([P, 8, 8, 64], BF16, name="R%d" % hh, align_bytes=64) for hh in range(2)]
+        R = [keep.tile([P, 8, 2, 128], F32, name="R%d" % hh, align_bytes=64) for hh in range(2)]
         G = [keep.tile([P, 8, 128, 2], F32, name="G%d" % hh, align_bytes=64) for hh in range(2)]
         a_codes = [keep.tile([P, 1024], U32, name="ac%d" % hh, align_bytes=64) for hh in range(2)]
         a_scales = [keep.tile([P, 1024], U8, name="as%d" % hh, align_bytes=64) for hh in range(2)]
@@ -73,7 +70,6 @@ def tile_reasoningmultiheadattention_pb_kernel(tc, h_attn, Wo, bo, out_0, out_1)
         ident = keep.tile([P, P], F32, name="ident")
         perm = keep.tile([P, P], F32, name="perm")
         ones = keep.tile([P, P], BF16, name="ones")
-        identb = keep.tile([P, P], BF16, name="identb")
         brow = keep.tile([P, 1024], BF16, name="brow")
         bias = keep.tile([P, 1024], F32, name="bias")
         banks = {}
@@ -92,11 +88,17 @@ def tile_reasoningmultiheadattention_pb_kernel(tc, h_attn, Wo, bo, out_0, out_1)
 
         nc.gpsimd.memset(ones[:], 1.0)
         make_identity(nc, ident[:])
-        make_identity(nc, identb[:])
         nc.vector.tensor_copy(
             out=perm[:].rearrange("p (g b q) -> p g b q", g=2, b=4),
             in_=ident[:].rearrange("p (b q g) -> p g b q", b=4, g=2),
         )
+
+        warm_src = (T[0][:, 0, :], Wraw[(0, 1)][:, 0, :], Wraw[(1, 0)][:, 0, :], Wraw[(1, 1)][:, 0, :])
+
+        def op_dm(i):
+            scratch = tps.tile([P, 512], F32, name="scratch", tag="tp")
+            for s in range(2):
+                nc.tensor.matmul(out=scratch[:], lhsT=ones[:], rhs=warm_src[i], start=True, stop=True)
 
         def op_bm(nh):
             banks[("b", nh)] = accs.tile([P, 512], F32, name="acc")
@@ -108,27 +110,22 @@ def tile_reasoningmultiheadattention_pb_kernel(tc, h_attn, Wo, bo, out_0, out_1)
             nc.scalar.copy(out=bias[:, 512 * nh : 512 * nh + 512], in_=banks[("b", nh)][:])
 
         def op_rl(hh, jh):
-            nc.vector.tensor_copy(
-                out=R[hh][:, :, 4 * jh : 4 * jh + 4, :],
-                in_=T[hh][:, 4 * jh : 4 * jh + 4, :].rearrange("p j (h d) -> p h j d", d=64),
-            )
+            tw = T[hh][:].rearrange("p j c -> p (j c)").bitcast(F32).rearrange("p (j h e u) -> p h u j e", j=8, h=8, u=2)
+            rv = R[hh][:].rearrange("p h u (j e) -> p h u j e", j=8)
+            nc.vector.tensor_copy(out=rv[:, :, :, 4 * jh : 4 * jh + 4, :], in_=tw[:, :, :, 4 * jh : 4 * jh + 4, :])
 
         def op_tr(hh, hp):
-            rw = R[hh][:].rearrange("p h j d -> p (h j d)").bitcast(F32)
             pt = tps.tile([P, 2, 8, 2, 16], F32, name="pt", tag="tp")
             banks[("t", hh, hp)] = pt
             for hl in range(2):
                 for u in range(2):
-                    h = 2 * hp + hl
-                    nc.tensor.transpose(out=pt[:, u, :, hl, :], in_=rw[:, 256 * h + u : 256 * (h + 1) : 2], identity=perm[:])
+                    nc.tensor.transpose(out=pt[:, u, :, hl, :], in_=R[hh][:, 2 * hp + hl, u, :], identity=perm[:])
 
         def op_yc(hh, hp):
-            dst = G[hh][:, :, 32 * hp : 32 * hp + 32, :]
-            src = banks[("t", hh, hp)][:].rearrange("p u a hl q -> p a (hl q) u")
-            if "%d%d" % (hh, hp) in V_YC:
-                nc.vector.tensor_copy(out=dst, in_=src)
-            else:
-                nc.scalar.copy(out=dst, in_=src)
+            nc.scalar.copy(
+                out=G[hh][:, :, 32 * hp : 32 * hp + 32, :],
+                in_=banks[("t", hh, hp)][:].rearrange("p u a hl q -> p a (hl q) u"),
+            )
 
         def op_yq(hh, g):
             gb = G[hh][:].rearrange("p a m u -> p (a m u)").bitcast(BF16)
@@ -143,30 +140,6 @@ def tile_reasoningmultiheadattention_pb_kernel(tc, h_attn, Wo, bo, out_0, out_1)
 
         def op_ws(nh, g):
             nc.scalar.copy(out=Wg[(nh, g)][:], in_=Wraw[(nh, g)][:].rearrange("p t c -> p c t"))
-
-        def op_wh(nh, g, k):
-            src = Wraw[(nh, g)][:].rearrange("p t c -> p c t")
-            if "%d%d%d" % (nh, g, k) in S_WH:
-                nc.scalar.copy(out=Wg[(nh, g)][:, 256 * k : 256 * k + 256, :], in_=src[:, 256 * k : 256 * k + 256, :])
-            else:
-                nc.vector.tensor_copy(out=Wg[(nh, g)][:, 256 * k : 256 * k + 256, :], in_=src[:, 256 * k : 256 * k + 256, :])
-
-        def op_wm(nh, g, k):
-            src = Wraw[(nh, g)][:].rearrange("p t c -> p c t")
-            pw = tps.tile([P, 256, 4], BF16, name="pw", tag="tp")
-            banks[("w", nh, g, k)] = pw
-            for s in range(2):
-                c0 = 256 * k + 128 * s
-                nc.tensor.matmul(
-                    out=pw[:, 128 * s : 128 * s + 128, :], lhsT=identb[:], rhs=src[:, c0 : c0 + 128, :], start=True, stop=True
-                )
-
-        def op_wc(nh, g, k):
-            dst = Wg[(nh, g)][:, 256 * k : 256 * k + 256, :]
-            if "%d%d%d" % (nh, g, k) in V_WC:
-                nc.vector.tensor_copy(out=dst, in_=banks[("w", nh, g, k)][:])
-            else:
-                nc.scalar.copy(out=dst, in_=banks[("w", nh, g, k)][:])
 
         def op_wq(nh, g):
             nc.vector.quantize_mx(
@@ -212,8 +185,8 @@ def tile_reasoningmultiheadattention_pb_kernel(tc, h_attn, Wo, bo, out_0, out_1)
             nc.sync.dma_start(out=out_1[b, 128 * hh : 128 * hh + 128, :], in_=o1[(hh, b)][:].bitcast(U8))
 
         table = {
-            "bm": op_bm, "bc": op_bc, "rl": op_rl, "tr": op_tr, "yc": op_yc, "yq": op_yq, "wv": op_wv, "ws": op_ws,
-            "wh": op_wh, "wm": op_wm, "wc": op_wc, "wq": op_wq, "mx": op_mx, "ad": op_ad, "s0": op_s0, "ca": op_ca, "s1": op_s1,
+            "dm": op_dm, "bm": op_bm, "bc": op_bc, "rl": op_rl, "tr": op_tr, "yc": op_yc, "yq": op_yq, "wv": op_wv,
+            "ws": op_ws, "wq": op_wq, "mx": op_mx, "ad": op_ad, "s0": op_s0, "ca": op_ca, "s1": op_s1,
         }
         for step in ORDER:
             table[step[:2]](*[int(c) for c in step[2:]])

@@ -12,27 +12,25 @@ U8 = mybir.dt.uint8
 FP8X4 = mybir.dt.float8_e4m3fn_x4
 FP8 = mybir.dt.float8_e4m3fn
 ADD = mybir.AluOpType.add
-MULT = mybir.AluOpType.mult
 COPY = mybir.ActivationFunctionType.Copy
 
 P = 128
 Y_SCALE = 400.0
 
 LOADS = ("y00", "y01", "b", "w00", "w01", "w10", "w11", "y10", "y11")
-V_CASTS = ()
 ORDER = (
     "dm0", "rl00", "rl01", "bm0", "bm1", "bc0", "tr00", "bc1", "tr01", "wv00",
-    "tr02", "yc00", "yc01", "tr03", "yc02", "wv01", "dm1", "yc03", "wq00", "ws10",
-    "dm2", "wq01", "yq00", "dm3", "yq01", "ws11", "wq10", "mx000", "mx010", "rl10",
-    "mx020", "ad000", "mx030", "rl11", "ca000", "ad010", "tr10", "s0000", "tr11", "wq11",
-    "yc10", "tr12", "ad020", "yc11", "s0010", "mx001", "ad030", "yc12", "tr13", "ad001",
-    "ca010", "mx011", "s0020", "yc13", "mx021", "s0030", "ad011", "ca020", "mx031", "s0001",
-    "yq10", "ca030", "yq11", "s0011", "ca001", "ad021", "mx100", "ca011", "ad031", "mx110",
-    "ca021", "s100", "ad100", "mx120", "s0021", "ca031", "mx130", "ad110", "s101", "ca100",
-    "s0031", "mx101", "ad120", "ca110", "mx111", "s102", "ad130", "ca120", "s0100", "mx121",
-    "ad101", "ca130", "s103", "mx131", "ad111", "s0110", "ca101", "ad121", "s0120", "ca111",
-    "ad131", "s0130", "ca121", "s0101", "ca131", "s0111", "s110", "s0121", "s111", "s0131",
-    "s112", "s113",
+    "tr02", "yc00", "yc01", "tr03", "yc02", "yq00", "dm1", "wq00", "yc03", "wv01",
+    "dm2", "ws10", "yq01", "wq01", "dm3", "yq02", "mx000", "yq03", "ws11", "mx010",
+    "wq10", "mx020", "rl10", "mx030", "ad000", "rl11", "ca000", "ad010", "tr10", "s0000",
+    "tr11", "wq11", "yc10", "tr12", "ad020", "yc11", "s0010", "mx001", "ad030", "yc12",
+    "tr13", "ad001", "ca010", "mx011", "s0020", "yq10", "yc13", "mx021", "s0030", "ad011",
+    "ca020", "mx031", "s0001", "ad021", "ca030", "mx100", "ad031", "s0011", "mx101", "ca001",
+    "ad100", "s0021", "ca011", "ad101", "s0031", "ca021", "yq11", "ca031", "s100", "yq12",
+    "mx110", "s101", "yq13", "ca100", "s010", "mx111", "ad110", "ca101", "mx120", "ad111",
+    "ca110", "s102", "mx121", "ad120", "s103", "ca111", "mx130", "s110", "ad121", "s011",
+    "ca120", "mx131", "ad130", "ca121", "ad131", "s111", "ca130", "s012", "ca131", "s112",
+    "s013", "s113",
 )
 
 
@@ -49,9 +47,9 @@ def tile_reasoningmultiheadattention_pb_kernel(tc, h_attn, Wo, bo, out_0, out_1)
 
         T = [keep.tile([P, 8, 512], BF16, name="T%d" % hh) for hh in range(2)]
         R = [keep.tile([P, 8, 2, 128], F32, name="R%d" % hh, align_bytes=64) for hh in range(2)]
-        G = [keep.tile([P, 8, 128, 2], F32, name="G%d" % hh, align_bytes=64) for hh in range(2)]
-        a_codes = [keep.tile([P, 1024], U32, name="ac%d" % hh, align_bytes=64) for hh in range(2)]
-        a_scales = [keep.tile([P, 1024], U8, name="as%d" % hh, align_bytes=64) for hh in range(2)]
+        G = [keep.tile([P, 2, 128, 2], F32, name="G%d" % t, align_bytes=64) for t in range(8)]
+        a_codes = [keep.tile([P, 256], U32, name="ac%d" % t, align_bytes=64) for t in range(8)]
+        a_scales = [keep.tile([P, 256], U8, name="as%d" % t, align_bytes=64) for t in range(8)]
         Wraw = {}
         Wg = {}
         for nh in range(2):
@@ -60,12 +58,8 @@ def tile_reasoningmultiheadattention_pb_kernel(tc, h_attn, Wo, bo, out_0, out_1)
                 Wg[(nh, g)] = keep.tile([P, 512, 4], BF16, name="wg%d%d" % (nh, g), align_bytes=64)
         b_codes = [keep.tile([P, 1024], U32, name="bc%d" % g, align_bytes=64) for g in range(2)]
         b_scales = [keep.tile([P, 1024], U8, name="bs%d" % g, align_bytes=64) for g in range(2)]
-        o0 = {}
-        o1 = {}
-        for hh in range(2):
-            for b in range(4):
-                o0[(hh, b)] = keep.tile([P, 1024], F32, name="o0_%d%d" % (hh, b))
-                o1[(hh, b)] = keep.tile([P, 1024], FP8, name="o1_%d%d" % (hh, b))
+        o0 = [keep.tile([P, 1024], F32, name="o0_%d" % t) for t in range(8)]
+        o1 = [keep.tile([P, 1024], FP8, name="o1_%d" % t) for t in range(8)]
 
         ident = keep.tile([P, P], F32, name="ident")
         perm = keep.tile([P, P], F32, name="perm")
@@ -89,8 +83,8 @@ def tile_reasoningmultiheadattention_pb_kernel(tc, h_attn, Wo, bo, out_0, out_1)
         nc.gpsimd.memset(ones[:], 1.0)
         make_identity(nc, ident[:])
         nc.vector.tensor_copy(
-            out=perm[:].rearrange("p (g b q) -> p g b q", g=2, b=4),
-            in_=ident[:].rearrange("p (b q g) -> p g b q", b=4, g=2),
+            out=perm[:].rearrange("p (g q b) -> p g q b", g=2, b=4),
+            in_=ident[:].rearrange("p (b q g) -> p g q b", b=4, g=2),
         )
 
         warm_src = (T[0][:, 0, :], Wraw[(0, 1)][:, 0, :], Wraw[(1, 0)][:, 0, :], Wraw[(1, 1)][:, 0, :])
@@ -115,24 +109,21 @@ def tile_reasoningmultiheadattention_pb_kernel(tc, h_attn, Wo, bo, out_0, out_1)
             nc.vector.tensor_copy(out=rv[:, :, :, 4 * jh : 4 * jh + 4, :], in_=tw[:, :, :, 4 * jh : 4 * jh + 4, :])
 
         def op_tr(hh, hp):
-            pt = tps.tile([P, 2, 8, 2, 16], F32, name="pt", tag="tp")
+            pt = tps.tile([P, 2, 2, 2, 64], F32, name="pt", tag="tp")
             banks[("t", hh, hp)] = pt
             for hl in range(2):
                 for u in range(2):
                     nc.tensor.transpose(out=pt[:, u, :, hl, :], in_=R[hh][:, 2 * hp + hl, u, :], identity=perm[:])
 
         def op_yc(hh, hp):
-            nc.scalar.copy(
-                out=G[hh][:, :, 32 * hp : 32 * hp + 32, :],
-                in_=banks[("t", hh, hp)][:].rearrange("p u a hl q -> p a (hl q) u"),
-            )
+            nc.scalar.copy(out=G[4 * hh + hp][:], in_=banks[("t", hh, hp)][:].rearrange("p u g hl x -> p g (hl x) u"))
 
-        def op_yq(hh, g):
-            gb = G[hh][:].rearrange("p a m u -> p (a m u)").bitcast(BF16)
+        def op_yq(hh, hp):
+            t = 4 * hh + hp
             nc.vector.quantize_mx(
-                out=a_codes[hh][:, 512 * g : 512 * g + 512].bitcast(FP8X4),
-                scales=a_scales[hh][:, 512 * g : 512 * g + 512],
-                in_=gb[:, 2048 * g : 2048 * g + 2048],
+                out=a_codes[t][:].bitcast(FP8X4),
+                scales=a_scales[t][:],
+                in_=G[t][:].rearrange("p g m u -> p (g m u)").bitcast(BF16),
             )
 
         def op_wv(nh, g):
@@ -148,41 +139,40 @@ def tile_reasoningmultiheadattention_pb_kernel(tc, h_attn, Wo, bo, out_0, out_1)
                 in_=Wg[(nh, g)][:].rearrange("p c t -> p (c t)"),
             )
 
-        def op_mx(hh, b, nh):
+        def op_mx(hh, hp, nh):
+            t = 4 * hh + hp
             cols = slice(512 * nh, 512 * nh + 512)
             acc = accs.tile([P, 512], F32, name="acc")
-            banks[("m", hh, b, nh)] = acc
+            banks[("m", t, nh)] = acc
             for g in range(2):
-                a = 4 * g + b
                 nc.tensor.matmul_mx(
                     out=acc[:],
-                    lhsT=a_codes[hh][:, 128 * a : 128 * a + 128].bitcast(FP8X4),
-                    lhsT_scale=a_scales[hh][:, 128 * a : 128 * a + 128],
+                    lhsT=a_codes[t][:, 128 * g : 128 * g + 128].bitcast(FP8X4),
+                    lhsT_scale=a_scales[t][:, 128 * g : 128 * g + 128],
                     rhs=b_codes[g][:, cols].bitcast(FP8X4),
                     rhs_scale=b_scales[g][:, cols],
                     start=(g == 0),
                     stop=(g == 1),
                 )
 
-        def op_ad(hh, b, nh):
+        def op_ad(hh, hp, nh):
+            t = 4 * hh + hp
             cols = slice(512 * nh, 512 * nh + 512)
-            nc.vector.tensor_tensor(out=o0[(hh, b)][:, cols], in0=banks[("m", hh, b, nh)][:], in1=bias[:, cols], op=ADD)
+            nc.vector.tensor_tensor(out=o0[t][:, cols], in0=banks[("m", t, nh)][:], in1=bias[:, cols], op=ADD)
 
-        def op_s0(hh, b, nh):
+        def op_s0(hh, hp, nh=2):
+            t = 4 * hh + hp
+            cols = slice(0, 1024) if nh == 2 else slice(512 * nh, 512 * nh + 512)
+            nc.sync.dma_start(out=out_0[:, 32 * t : 32 * t + 32, cols].rearrange("b r n -> r b n"), in_=o0[t][:, cols])
+
+        def op_ca(hh, hp, nh):
+            t = 4 * hh + hp
             cols = slice(512 * nh, 512 * nh + 512)
-            nc.sync.dma_start(out=out_0[b, 128 * hh : 128 * hh + 128, cols], in_=o0[(hh, b)][:, cols])
+            nc.scalar.activation(out=o1[t][:, cols], in_=o0[t][:, cols], func=COPY, scale=Y_SCALE, saturate=False)
 
-        def op_ca(hh, b, nh):
-            cols = slice(512 * nh, 512 * nh + 512)
-            if "%d%d%d" % (hh, b, nh) in V_CASTS:
-                nc.vector.tensor_scalar(
-                    out=o1[(hh, b)][:, cols], in0=o0[(hh, b)][:, cols], scalar1=Y_SCALE, scalar2=None, op0=MULT, saturate=False
-                )
-            else:
-                nc.scalar.activation(out=o1[(hh, b)][:, cols], in_=o0[(hh, b)][:, cols], func=COPY, scale=Y_SCALE, saturate=False)
-
-        def op_s1(hh, b):
-            nc.sync.dma_start(out=out_1[b, 128 * hh : 128 * hh + 128, :], in_=o1[(hh, b)][:].bitcast(U8))
+        def op_s1(hh, hp):
+            t = 4 * hh + hp
+            nc.sync.dma_start(out=out_1[:, 32 * t : 32 * t + 32, :].rearrange("b r n -> r b n"), in_=o1[t][:].bitcast(U8))
 
         table = {
             "dm": op_dm, "bm": op_bm, "bc": op_bc, "rl": op_rl, "tr": op_tr, "yc": op_yc, "yq": op_yq, "wv": op_wv,

@@ -127,10 +127,16 @@ def tile_reasoningmultiheadattention_pb_kernel(tc, h_attn, Wo, bo, out_0, out_1)
             )
 
         def op_wv(nh, g):
-            nc.vector.tensor_copy(out=Wg[(nh, g)][:], in_=Wraw[(nh, g)][:].rearrange("p t c -> p c t"))
+            nc.vector.tensor_copy(
+                out=Wg[(nh, g)][:].rearrange("p (c i) t -> p c t i", i=4),
+                in_=Wraw[(nh, g)][:].rearrange("p t (c i) -> p c t i", i=4),
+            )
 
         def op_ws(nh, g):
-            nc.scalar.copy(out=Wg[(nh, g)][:], in_=Wraw[(nh, g)][:].rearrange("p t c -> p c t"))
+            nc.scalar.copy(
+                out=Wg[(nh, g)][:].rearrange("p (c i) t -> p c t i", i=4),
+                in_=Wraw[(nh, g)][:].rearrange("p t (c i) -> p c t i", i=4),
+            )
 
         def op_wq(nh, g):
             nc.vector.quantize_mx(

@@ -16,69 +16,68 @@ COPY = mybir.ActivationFunctionType.Copy
 
 P = 128
 Y_SCALE = 400.0
-
-LOADS = ("y00", "y01", "b", "w00", "w01", "w10", "w11", "y10", "y11")
-ORDER = (
-    "dm0", "rl00", "rl01", "bm0", "bm1", "bc0", "tr00", "bc1", "tr01", "wv00",
-    "tr02", "yc00", "yc01", "tr03", "yc02", "yq00", "dm1", "wq00", "yc03", "wv01",
-    "dm2", "ws10", "yq01", "wq01", "dm3", "yq02", "mx000", "yq03", "ws11", "mx010",
-    "wq10", "mx020", "rl10", "mx030", "ad000", "rl11", "ca000", "ad010", "tr10", "s0000",
-    "tr11", "wq11", "yc10", "tr12", "ad020", "yc11", "s0010", "mx001", "ad030", "yc12",
-    "tr13", "ad001", "ca010", "mx011", "s0020", "yq10", "yc13", "mx021", "s0030", "ad011",
-    "ca020", "mx031", "s0001", "ad021", "ca030", "mx100", "ad031", "s0011", "mx101", "ca001",
-    "ad100", "s0021", "ca011", "ad101", "s0031", "ca021", "yq11", "ca031", "s100", "yq12",
-    "mx110", "s101", "yq13", "ca100", "s010", "mx111", "ad110", "ca101", "mx120", "ad111",
-    "ca110", "s102", "mx121", "ad120", "s103", "ca111", "mx130", "s110", "ad121", "s011",
-    "ca120", "mx131", "ad130", "ca121", "ad131", "s111", "ca130", "s012", "ca131", "s112",
-    "s013", "s113",
-)
+PASSES = 2
+HALF = 512
+TILES = 8
+ROWS = 32
+TURN_BANKS = 3
+SUM_BANKS = 5
+TURN_LEAD = 2
 
 
 def tile_reasoningmultiheadattention_pb_kernel(tc, h_attn, Wo, bo, out_0, out_1):
     nc = tc.nc
     with ExitStack() as ctx:
         keep = ctx.enter_context(tc.tile_pool(name="keep", bufs=1))
-        tps = ctx.enter_context(tc.psum_pool(name="tps", bufs=3))
-        accs = ctx.enter_context(tc.psum_pool(name="accs", bufs=5))
+        turn_banks = ctx.enter_context(tc.psum_pool(name="turn_banks", bufs=TURN_BANKS))
+        sum_banks = ctx.enter_context(tc.psum_pool(name="sum_banks", bufs=SUM_BANKS))
         ctx.enter_context(tc.manual_schedule())
 
-        yv = h_attn.rearrange("b (x j) h d -> (b x) j (h d)", j=8)
-        wv = Wo.rearrange("(g p t) n -> g p t n", g=2, t=4)
+        y_hbm = h_attn.rearrange("b (x j) h d -> (b x) j (h d)", j=8)
+        w_hbm = Wo.rearrange("(g p t) n -> g p t n", g=PASSES, t=4)
 
-        T = [keep.tile([P, 8, 512], BF16, name="T%d" % hh) for hh in range(2)]
-        R = [keep.tile([P, 8, 2, 128], F32, name="R%d" % hh, align_bytes=64) for hh in range(2)]
-        G = [keep.tile([P, 2, 128, 2], F32, name="G%d" % t, align_bytes=64) for t in range(8)]
-        a_codes = [keep.tile([P, 256], U32, name="ac%d" % t, align_bytes=64) for t in range(8)]
-        a_scales = [keep.tile([P, 256], U8, name="as%d" % t, align_bytes=64) for t in range(8)]
-        Wraw = {}
-        Wg = {}
+        y_raw = [keep.tile([P, 8, 512], BF16, name="y_raw%d" % hh) for hh in range(2)]
+        y_heads = [keep.tile([P, 8, 2, 128], F32, name="y_heads%d" % hh, align_bytes=64) for hh in range(2)]
+        y_grouped = [keep.tile([P, PASSES, 128, 2], F32, name="y_grouped%d" % t, align_bytes=64) for t in range(TILES)]
+        y_codes = [keep.tile([P, PASSES * 128], U32, name="y_codes%d" % t, align_bytes=64) for t in range(TILES)]
+        y_scales = [keep.tile([P, PASSES * 128], U8, name="y_scales%d" % t, align_bytes=64) for t in range(TILES)]
+        w_raw = {}
+        w_grouped = {}
         for nh in range(2):
-            for g in range(2):
-                Wraw[(nh, g)] = keep.tile([P, 4, 512], BF16, name="wr%d%d" % (nh, g))
-                Wg[(nh, g)] = keep.tile([P, 512, 4], BF16, name="wg%d%d" % (nh, g), align_bytes=64)
-        b_codes = [keep.tile([P, 1024], U32, name="bc%d" % g, align_bytes=64) for g in range(2)]
-        b_scales = [keep.tile([P, 1024], U8, name="bs%d" % g, align_bytes=64) for g in range(2)]
-        o0 = [keep.tile([P, 1024], F32, name="o0_%d" % t) for t in range(8)]
-        o1 = [keep.tile([P, 1024], FP8, name="o1_%d" % t) for t in range(8)]
+            for g in range(PASSES):
+                w_raw[(nh, g)] = keep.tile([P, 4, HALF], BF16, name="w_raw%d%d" % (nh, g))
+                w_grouped[(nh, g)] = keep.tile([P, HALF, 4], BF16, name="w_grouped%d%d" % (nh, g), align_bytes=64)
+        w_codes = [keep.tile([P, 2 * HALF], U32, name="w_codes%d" % g, align_bytes=64) for g in range(PASSES)]
+        w_scales = [keep.tile([P, 2 * HALF], U8, name="w_scales%d" % g, align_bytes=64) for g in range(PASSES)]
+        res = [keep.tile([P, 2 * HALF], F32, name="res%d" % t) for t in range(TILES)]
+        res_fp8 = [keep.tile([P, 2 * HALF], FP8, name="res_fp8_%d" % t) for t in range(TILES)]
 
         ident = keep.tile([P, P], F32, name="ident")
         perm = keep.tile([P, P], F32, name="perm")
         ones = keep.tile([P, P], BF16, name="ones")
-        brow = keep.tile([P, 1024], BF16, name="brow")
-        bias = keep.tile([P, 1024], F32, name="bias")
-        banks = {}
+        bias_row = keep.tile([P, 2 * HALF], BF16, name="bias_row")
+        bias = keep.tile([P, 2 * HALF], F32, name="bias")
+        bank_of = {}
 
-        nc.vector.memset(brow[:], 0.0)
-        for ld in LOADS:
-            if ld == "b":
-                nc.sync.dma_start(out=brow[0:1, :], in_=bo.rearrange("(o n) -> o n", o=1))
-                continue
-            i = int(ld[1])
-            k = int(ld[2])
-            if ld[0] == "y":
-                nc.sync.dma_start(out=T[i][:, 4 * k : 4 * k + 4, :], in_=yv[:, 4 * k : 4 * k + 4, 512 * i : 512 * i + 512])
-            else:
-                nc.sync.dma_start(out=Wraw[(i, k)][:], in_=wv[k][:, :, 512 * i : 512 * i + 512])
+        def halfcols(nh):
+            return slice(HALF * nh, HALF * nh + HALF)
+
+        def load_y(hh, jh):
+            tokens = slice(4 * jh, 4 * jh + 4)
+            nc.sync.dma_start(out=y_raw[hh][:, tokens, :], in_=y_hbm[:, tokens, 512 * hh : 512 * hh + 512])
+
+        def load_w(nh, g):
+            nc.sync.dma_start(out=w_raw[(nh, g)][:], in_=w_hbm[g][:, :, halfcols(nh)])
+
+        nc.vector.memset(bias_row[:], 0.0)
+        load_y(0, 0)
+        load_y(0, 1)
+        nc.sync.dma_start(out=bias_row[0:1, :], in_=bo.rearrange("(o n) -> o n", o=1))
+        for nh in range(2):
+            for g in range(PASSES):
+                load_w(nh, g)
+        load_y(1, 0)
+        load_y(1, 1)
 
         nc.gpsimd.memset(ones[:], 1.0)
         make_identity(nc, ident[:])
@@ -87,102 +86,168 @@ def tile_reasoningmultiheadattention_pb_kernel(tc, h_attn, Wo, bo, out_0, out_1)
             in_=ident[:].rearrange("p (b q g) -> p g q b", b=4, g=2),
         )
 
-        warm_src = (T[0][:, 0, :], Wraw[(0, 1)][:, 0, :], Wraw[(1, 0)][:, 0, :], Wraw[(1, 1)][:, 0, :])
+        def keep_tensor_busy(loaded):
+            unread = turn_banks.tile([P, HALF], F32, name="unread", tag="turn")
+            for repeat in range(2):
+                nc.tensor.matmul(out=unread[:], lhsT=ones[:], rhs=loaded, start=True, stop=True)
 
-        def op_dm(i):
-            scratch = tps.tile([P, 512], F32, name="scratch", tag="tp")
-            for s in range(2):
-                nc.tensor.matmul(out=scratch[:], lhsT=ones[:], rhs=warm_src[i], start=True, stop=True)
-
-        def op_bm(nh):
-            banks[("b", nh)] = accs.tile([P, 512], F32, name="acc")
+        def spread_bias(nh):
+            bank_of[("bias", nh)] = sum_banks.tile([P, HALF], F32, name="sums")
             nc.tensor.matmul(
-                out=banks[("b", nh)][:], lhsT=ones[:], rhs=brow[:, 512 * nh : 512 * nh + 512], start=True, stop=True
+                out=bank_of[("bias", nh)][:], lhsT=ones[:], rhs=bias_row[:, halfcols(nh)], start=True, stop=True
             )
 
-        def op_bc(nh):
-            nc.scalar.copy(out=bias[:, 512 * nh : 512 * nh + 512], in_=banks[("b", nh)][:])
+        def keep_bias(nh):
+            nc.scalar.copy(out=bias[:, halfcols(nh)], in_=bank_of[("bias", nh)][:])
 
-        def op_rl(hh, jh):
-            tw = T[hh][:].rearrange("p j c -> p (j c)").bitcast(F32).rearrange("p (j h e u) -> p h u j e", j=8, h=8, u=2)
-            rv = R[hh][:].rearrange("p h u (j e) -> p h u j e", j=8)
-            nc.vector.tensor_copy(out=rv[:, :, :, 4 * jh : 4 * jh + 4, :], in_=tw[:, :, :, 4 * jh : 4 * jh + 4, :])
+        def regroup(hh, jh):
+            words = y_raw[hh][:].rearrange("p j c -> p (j c)").bitcast(F32)
+            src = words.rearrange("p (j h e u) -> p h u j e", j=8, h=8, u=2)
+            dst = y_heads[hh][:].rearrange("p h u (j e) -> p h u j e", j=8)
+            tokens = slice(4 * jh, 4 * jh + 4)
+            nc.vector.tensor_copy(out=dst[:, :, :, tokens, :], in_=src[:, :, :, tokens, :])
 
-        def op_tr(hh, hp):
-            pt = tps.tile([P, 2, 2, 2, 64], F32, name="pt", tag="tp")
-            banks[("t", hh, hp)] = pt
+        def turn(t):
+            hh, pair = divmod(t, 4)
+            bank = turn_banks.tile([P, 2, PASSES, 2, 64], F32, name="turned", tag="turn")
+            bank_of[("turned", t)] = bank
             for hl in range(2):
                 for u in range(2):
-                    nc.tensor.transpose(out=pt[:, u, :, hl, :], in_=R[hh][:, 2 * hp + hl, u, :], identity=perm[:])
+                    nc.tensor.transpose(out=bank[:, u, :, hl, :], in_=y_heads[hh][:, 2 * pair + hl, u, :], identity=perm[:])
 
-        def op_yc(hh, hp):
-            nc.scalar.copy(out=G[4 * hh + hp][:], in_=banks[("t", hh, hp)][:].rearrange("p u g hl x -> p g (hl x) u"))
+        def unload(t):
+            nc.scalar.copy(out=y_grouped[t][:], in_=bank_of[("turned", t)][:].rearrange("p u g hl x -> p g (hl x) u"))
 
-        def op_yq(hh, hp):
-            t = 4 * hh + hp
+        def quantize_y(t):
             nc.vector.quantize_mx(
-                out=a_codes[t][:].bitcast(FP8X4),
-                scales=a_scales[t][:],
-                in_=G[t][:].rearrange("p g m u -> p (g m u)").bitcast(BF16),
+                out=y_codes[t][:].bitcast(FP8X4),
+                scales=y_scales[t][:],
+                in_=y_grouped[t][:].rearrange("p g m u -> p (g m u)").bitcast(BF16),
             )
 
-        def op_wv(nh, g):
-            nc.vector.tensor_copy(
-                out=Wg[(nh, g)][:].rearrange("p (c i) t -> p c t i", i=4),
-                in_=Wraw[(nh, g)][:].rearrange("p t (c i) -> p c t i", i=4),
+        def interleave_w(copy, nh, g):
+            copy(
+                out=w_grouped[(nh, g)][:].rearrange("p (c i) t -> p c t i", i=4),
+                in_=w_raw[(nh, g)][:].rearrange("p t (c i) -> p c t i", i=4),
             )
 
-        def op_ws(nh, g):
-            nc.scalar.copy(
-                out=Wg[(nh, g)][:].rearrange("p (c i) t -> p c t i", i=4),
-                in_=Wraw[(nh, g)][:].rearrange("p t (c i) -> p c t i", i=4),
-            )
-
-        def op_wq(nh, g):
+        def quantize_w(nh, g):
             nc.vector.quantize_mx(
-                out=b_codes[g][:, 512 * nh : 512 * nh + 512].bitcast(FP8X4),
-                scales=b_scales[g][:, 512 * nh : 512 * nh + 512],
-                in_=Wg[(nh, g)][:].rearrange("p c t -> p (c t)"),
+                out=w_codes[g][:, halfcols(nh)].bitcast(FP8X4),
+                scales=w_scales[g][:, halfcols(nh)],
+                in_=w_grouped[(nh, g)][:].rearrange("p c t -> p (c t)"),
             )
 
-        def op_mx(hh, hp, nh):
-            t = 4 * hh + hp
-            cols = slice(512 * nh, 512 * nh + 512)
-            acc = accs.tile([P, 512], F32, name="acc")
-            banks[("m", t, nh)] = acc
-            for g in range(2):
+        def multiply(t, nh):
+            sums = sum_banks.tile([P, HALF], F32, name="sums")
+            bank_of[("sums", t, nh)] = sums
+            for g in range(PASSES):
+                of_pass = slice(128 * g, 128 * g + 128)
                 nc.tensor.matmul_mx(
-                    out=acc[:],
-                    lhsT=a_codes[t][:, 128 * g : 128 * g + 128].bitcast(FP8X4),
-                    lhsT_scale=a_scales[t][:, 128 * g : 128 * g + 128],
-                    rhs=b_codes[g][:, cols].bitcast(FP8X4),
-                    rhs_scale=b_scales[g][:, cols],
+                    out=sums[:],
+                    lhsT=y_codes[t][:, of_pass].bitcast(FP8X4),
+                    lhsT_scale=y_scales[t][:, of_pass],
+                    rhs=w_codes[g][:, halfcols(nh)].bitcast(FP8X4),
+                    rhs_scale=w_scales[g][:, halfcols(nh)],
                     start=(g == 0),
-                    stop=(g == 1),
+                    stop=(g == PASSES - 1),
                 )
 
-        def op_ad(hh, hp, nh):
-            t = 4 * hh + hp
-            cols = slice(512 * nh, 512 * nh + 512)
-            nc.vector.tensor_tensor(out=o0[t][:, cols], in0=banks[("m", t, nh)][:], in1=bias[:, cols], op=ADD)
+        def add_bias(t, nh):
+            nc.vector.tensor_tensor(out=res[t][:, halfcols(nh)], in0=bank_of[("sums", t, nh)][:], in1=bias[:, halfcols(nh)], op=ADD)
 
-        def op_s0(hh, hp, nh=2):
-            t = 4 * hh + hp
-            cols = slice(0, 1024) if nh == 2 else slice(512 * nh, 512 * nh + 512)
-            nc.sync.dma_start(out=out_0[:, 32 * t : 32 * t + 32, cols].rearrange("b r n -> r b n"), in_=o0[t][:, cols])
+        def cast_bytes(t, nh):
+            nc.scalar.activation(
+                out=res_fp8[t][:, halfcols(nh)], in_=res[t][:, halfcols(nh)], func=COPY, scale=Y_SCALE, saturate=False
+            )
 
-        def op_ca(hh, hp, nh):
-            t = 4 * hh + hp
-            cols = slice(512 * nh, 512 * nh + 512)
-            nc.scalar.activation(out=o1[t][:, cols], in_=o0[t][:, cols], func=COPY, scale=Y_SCALE, saturate=False)
+        def store_floats(t, cols):
+            rows = slice(ROWS * t, ROWS * t + ROWS)
+            nc.sync.dma_start(out=out_0[:, rows, cols].rearrange("b r n -> r b n"), in_=res[t][:, cols])
 
-        def op_s1(hh, hp):
-            t = 4 * hh + hp
-            nc.sync.dma_start(out=out_1[:, 32 * t : 32 * t + 32, :].rearrange("b r n -> r b n"), in_=o1[t][:].bitcast(U8))
+        def store_bytes(t):
+            rows = slice(ROWS * t, ROWS * t + ROWS)
+            nc.sync.dma_start(out=out_1[:, rows, :].rearrange("b r n -> r b n"), in_=res_fp8[t][:].bitcast(U8))
 
-        table = {
-            "dm": op_dm, "bm": op_bm, "bc": op_bc, "rl": op_rl, "tr": op_tr, "yc": op_yc, "yq": op_yq, "wv": op_wv,
-            "ws": op_ws, "wq": op_wq, "mx": op_mx, "ad": op_ad, "s0": op_s0, "ca": op_ca, "s1": op_s1,
-        }
-        for step in ORDER:
-            table[step[:2]](*[int(c) for c in step[2:]])
+        whole_rows = slice(0, 2 * HALF)
+
+        keep_tensor_busy(y_raw[0][:, 0, :])
+        regroup(0, 0)
+        regroup(0, 1)
+        for nh in range(2):
+            spread_bias(nh)
+        for nh in range(2):
+            keep_bias(nh)
+        for step in range(4 + TURN_LEAD):
+            if step < 4:
+                turn(step)
+            if step >= TURN_LEAD:
+                unload(step - TURN_LEAD)
+        for g in range(PASSES):
+            interleave_w(nc.vector.tensor_copy, 0, g)
+            quantize_y(g)
+            quantize_w(0, g)
+        quantize_y(2)
+        quantize_y(3)
+        for chunk in ((0, 1), (1, 0), (1, 1)):
+            keep_tensor_busy(w_raw[chunk][:, 0, :])
+        for g in range(PASSES):
+            interleave_w(nc.scalar.copy, 1, g)
+
+        for t in range(4):
+            multiply(t, 0)
+        quantize_w(1, 0)
+        regroup(1, 0)
+        add_bias(0, 0)
+        store_floats(0, halfcols(0))
+        cast_bytes(0, 0)
+        regroup(1, 1)
+        add_bias(1, 0)
+        store_floats(1, halfcols(0))
+        for t in range(4, 4 + TURN_BANKS):
+            turn(t)
+        for t in range(4, 4 + TURN_BANKS):
+            unload(t)
+        quantize_w(1, 1)
+        for t in (2, 3):
+            add_bias(t, 0)
+            store_floats(t, halfcols(0))
+        multiply(0, 1)
+        turn(7)
+        cast_bytes(1, 0)
+        unload(7)
+        for t in (2, 3):
+            cast_bytes(t, 0)
+        for t in (1, 2, 3):
+            multiply(t, 1)
+        add_bias(0, 1)
+        quantize_y(4)
+        for t in (1, 2, 3):
+            add_bias(t, 1)
+        for t in range(4):
+            store_floats(t, halfcols(1))
+            cast_bytes(t, 1)
+
+        for nh in range(2):
+            multiply(4, nh)
+        for nh in range(2):
+            add_bias(4, nh)
+        for t in (0, 1):
+            store_bytes(t)
+        store_floats(4, whole_rows)
+        for t in (2, 3):
+            store_bytes(t)
+        for t in (5, 6, 7):
+            quantize_y(t)
+        for nh in range(2):
+            cast_bytes(4, nh)
+        for t in (5, 6, 7):
+            for nh in range(2):
+                multiply(t, nh)
+            for nh in range(2):
+                add_bias(t, nh)
+            store_bytes(t - 1)
+            store_floats(t, whole_rows)
+            for nh in range(2):
+                cast_bytes(t, nh)
+        store_bytes(7)

@@ -70,14 +70,15 @@ def tile_reasoningmultiheadattention_pb_kernel(tc, h_attn, Wo, bo, out_0, out_1)
             nc.sync.dma_start(out=w_raw[(nh, g)][:], in_=w_hbm[g][:, :, halfcols(nh)])
 
         nc.vector.memset(bias_row[:], 0.0)
-        load_y(0, 0)
-        load_y(0, 1)
+        for g in range(PASSES):
+            load_w(0, g)
         nc.sync.dma_start(out=bias_row[0:1, :], in_=bo.rearrange("(o n) -> o n", o=1))
-        for nh in range(2):
-            for g in range(PASSES):
-                load_w(nh, g)
-        load_y(1, 0)
-        load_y(1, 1)
+        for jh in range(2):
+            load_y(0, jh)
+        for g in range(PASSES):
+            load_w(1, g)
+        for jh in range(2):
+            load_y(1, jh)
 
         nc.gpsimd.memset(ones[:], 1.0)
         make_identity(nc, ident[:])
@@ -171,83 +172,90 @@ def tile_reasoningmultiheadattention_pb_kernel(tc, h_attn, Wo, bo, out_0, out_1)
 
         whole_rows = slice(0, 2 * HALF)
 
+        def finish_half(t, nh):
+            add_bias(t, nh)
+            store_floats(t, halfcols(nh))
+
+        def finish_whole(t):
+            for nh in range(2):
+                add_bias(t, nh)
+            store_floats(t, whole_rows)
+
+        def multiply_tile(t):
+            for nh in range(2):
+                multiply(t, nh)
+
+        for nh in range(2):
+            spread_bias(nh)
+        interleave_w(nc.vector.tensor_copy, 0, 0)
+        interleave_w(nc.scalar.copy, 0, 1)
+        keep_tensor_busy(w_raw[(0, 1)][:, 0, :])
+        quantize_w(0, 0)
         keep_tensor_busy(y_raw[0][:, 0, :])
         regroup(0, 0)
         regroup(0, 1)
-        for nh in range(2):
-            spread_bias(nh)
-        for nh in range(2):
-            keep_bias(nh)
+        quantize_w(0, 1)
+        keep_bias(0)
         for step in range(4 + TURN_LEAD):
             if step < 4:
                 turn(step)
             if step >= TURN_LEAD:
                 unload(step - TURN_LEAD)
-        for g in range(PASSES):
-            interleave_w(nc.vector.tensor_copy, 0, g)
-            quantize_y(g)
-            quantize_w(0, g)
-        quantize_y(2)
-        quantize_y(3)
-        for chunk in ((0, 1), (1, 0), (1, 1)):
-            keep_tensor_busy(w_raw[chunk][:, 0, :])
-        for g in range(PASSES):
-            interleave_w(nc.scalar.copy, 1, g)
+        keep_tensor_busy(w_raw[(1, 0)][:, 0, :])
 
-        for t in range(4):
-            multiply(t, 0)
+        interleave_w(nc.vector.tensor_copy, 1, 0)
+        interleave_w(nc.scalar.copy, 1, 1)
+        quantize_y(0)
         quantize_w(1, 0)
+        quantize_y(1)
+        quantize_y(2)
+        for t in (0, 1):
+            multiply(t, 0)
         regroup(1, 0)
-        add_bias(0, 0)
-        store_floats(0, halfcols(0))
-        cast_bytes(0, 0)
+        quantize_y(3)
         regroup(1, 1)
-        add_bias(1, 0)
-        store_floats(1, halfcols(0))
-        for t in range(4, 4 + TURN_BANKS):
+        for t in (2, 3):
+            multiply(t, 0)
+        keep_bias(1)
+        for t in (0, 1):
+            finish_half(t, 0)
+        cast_bytes(0, 0)
+        for t in (4, 5, 6):
             turn(t)
-        for t in range(4, 4 + TURN_BANKS):
-            unload(t)
         quantize_w(1, 1)
         for t in (2, 3):
-            add_bias(t, 0)
-            store_floats(t, halfcols(0))
-        multiply(0, 1)
-        turn(7)
-        cast_bytes(1, 0)
-        unload(7)
-        for t in (2, 3):
-            cast_bytes(t, 0)
-        for t in (1, 2, 3):
-            multiply(t, 1)
-        add_bias(0, 1)
-        quantize_y(4)
-        for t in (1, 2, 3):
-            add_bias(t, 1)
+            finish_half(t, 0)
         for t in range(4):
-            store_floats(t, halfcols(1))
-            cast_bytes(t, 1)
-
-        for nh in range(2):
-            multiply(4, nh)
-        for nh in range(2):
-            add_bias(4, nh)
+            multiply(t, 1)
+        for t in (4, 5, 6):
+            unload(t)
+        turn(7)
         for t in (0, 1):
-            store_bytes(t)
-        store_floats(4, whole_rows)
-        for t in (2, 3):
-            store_bytes(t)
-        for t in (5, 6, 7):
-            quantize_y(t)
-        for nh in range(2):
-            cast_bytes(4, nh)
-        for t in (5, 6, 7):
+            finish_half(t, 1)
+        cast_bytes(1, 0)
+        cast_bytes(0, 1)
+        store_bytes(0)
+        quantize_y(4)
+        finish_half(2, 1)
+        cast_bytes(1, 1)
+        store_bytes(1)
+        unload(7)
+        quantize_y(5)
+        finish_half(3, 1)
+        multiply_tile(4)
+        quantize_y(6)
+        multiply_tile(5)
+
+        for t in range(4, 8):
             for nh in range(2):
-                multiply(t, nh)
-            for nh in range(2):
-                add_bias(t, nh)
-            store_bytes(t - 1)
-            store_floats(t, whole_rows)
+                cast_bytes(t - 2, nh)
+            store_bytes(t - 2)
+            finish_whole(t)
+            if t == 4:
+                quantize_y(7)
+            if t + 2 < TILES:
+                multiply_tile(t + 2)
+        for t in (6, 7):
             for nh in range(2):
                 cast_bytes(t, nh)
-        store_bytes(7)
+            store_bytes(t)

@@ -90,7 +90,7 @@ def tile_reasoningmultiheadattention_pb_kernel(tc, h_attn, Wo, bo, out_0, out_1)
         def keep_tensor_busy(loaded):
             unread = turn_banks.tile([P, HALF], F32, name="unread", tag="turn")
             for repeat in range(2):
-                nc.tensor.matmul(out=unread[:], lhsT=ones[:], rhs=loaded, start=True, stop=True)
+                nc.tensor.matmul(out=unread[:, 0:P], lhsT=ident[:], rhs=loaded.bitcast(F32)[:, 0:P], start=True, stop=True)
 
         def spread_bias(nh):
             bank_of[("bias", nh)] = sum_banks.tile([P, HALF], F32, name="sums")
@@ -185,22 +185,28 @@ def tile_reasoningmultiheadattention_pb_kernel(tc, h_attn, Wo, bo, out_0, out_1)
             for nh in range(2):
                 multiply(t, nh)
 
-        for nh in range(2):
-            spread_bias(nh)
+        keep_tensor_busy(w_raw[(0, 0)][:, 0, :])
         interleave_w(nc.vector.tensor_copy, 0, 0)
         interleave_w(nc.scalar.copy, 0, 1)
         keep_tensor_busy(w_raw[(0, 1)][:, 0, :])
+        for nh in range(2):
+            spread_bias(nh)
         quantize_w(0, 0)
         keep_tensor_busy(y_raw[0][:, 0, :])
         regroup(0, 0)
+        keep_tensor_busy(y_raw[0][:, 4, :])
         regroup(0, 1)
         quantize_w(0, 1)
         keep_bias(0)
-        for step in range(4 + TURN_LEAD):
-            if step < 4:
-                turn(step)
-            if step >= TURN_LEAD:
-                unload(step - TURN_LEAD)
+        for t in (0, 1):
+            turn(t)
+        unload(0)
+        turn(2)
+        unload(1)
+        keep_tensor_busy(y_raw[0][:, 4, :])
+        turn(3)
+        for t in (2, 3):
+            unload(t)
         keep_tensor_busy(w_raw[(1, 0)][:, 0, :])
 
         interleave_w(nc.vector.tensor_copy, 1, 0)

@@ -12,6 +12,7 @@ U8 = mybir.dt.uint8
 FP8X4 = mybir.dt.float8_e4m3fn_x4
 FP8 = mybir.dt.float8_e4m3fn
 ADD = mybir.AluOpType.add
+MULT = mybir.AluOpType.mult
 COPY = mybir.ActivationFunctionType.Copy
 
 P = 128
@@ -56,7 +57,7 @@ def tile_reasoningmultiheadattention_pb_kernel(tc, h_attn, Wo, bo, out_0, out_1)
         perm = keep.tile([P, P], F32, name="perm")
         ones = keep.tile([P, P], BF16, name="ones")
         bias_row = keep.tile([P, 2 * HALF], BF16, name="bias_row")
-        bias = keep.tile([P, 2 * HALF], F32, name="bias")
+        bias = keep.tile([P, 2 * HALF], BF16, name="bias")
         bank_of = {}
 
         def halfcols(nh):
@@ -93,13 +94,14 @@ def tile_reasoningmultiheadattention_pb_kernel(tc, h_attn, Wo, bo, out_0, out_1)
                 nc.tensor.matmul(out=unread[:, 0:P], lhsT=ident[:], rhs=loaded.bitcast(F32)[:, 0:P], start=True, stop=True)
 
         def spread_bias(nh):
-            bank_of[("bias", nh)] = sum_banks.tile([P, HALF], F32, name="sums")
+            if nh == 0:
+                bank_of["bias"] = sum_banks.tile([P, 2 * HALF], BF16, name="sums")
             nc.tensor.matmul(
-                out=bank_of[("bias", nh)][:], lhsT=ones[:], rhs=bias_row[:, halfcols(nh)], start=True, stop=True
+                out=bank_of["bias"][:, halfcols(nh)], lhsT=ones[:], rhs=bias_row[:, halfcols(nh)], start=True, stop=True
             )
 
-        def keep_bias(nh):
-            nc.scalar.copy(out=bias[:, halfcols(nh)], in_=bank_of[("bias", nh)][:])
+        def keep_bias():
+            nc.scalar.copy(out=bias[:], in_=bank_of["bias"][:])
 
         def regroup(hh, jh):
             words = y_raw[hh][:].rearrange("p j c -> p (j c)").bitcast(F32)
@@ -157,6 +159,11 @@ def tile_reasoningmultiheadattention_pb_kernel(tc, h_attn, Wo, bo, out_0, out_1)
         def add_bias(t, nh):
             nc.vector.tensor_tensor(out=res[t][:, halfcols(nh)], in0=bank_of[("sums", t, nh)][:], in1=bias[:, halfcols(nh)], op=ADD)
 
+        def cast_bytes_on_vector(t, nh):
+            nc.vector.tensor_scalar(
+                out=res_fp8[t][:, halfcols(nh)], in0=res[t][:, halfcols(nh)], scalar1=Y_SCALE, scalar2=None, op0=MULT, saturate=False
+            )
+
         def cast_bytes(t, nh):
             nc.scalar.activation(
                 out=res_fp8[t][:, halfcols(nh)], in_=res[t][:, halfcols(nh)], func=COPY, scale=Y_SCALE, saturate=False
@@ -197,7 +204,7 @@ def tile_reasoningmultiheadattention_pb_kernel(tc, h_attn, Wo, bo, out_0, out_1)
         keep_tensor_busy(y_raw[0][:, 4, :])
         regroup(0, 1)
         quantize_w(0, 1)
-        keep_bias(0)
+        keep_bias()
         for t in (0, 1):
             turn(t)
         unload(0)
@@ -219,12 +226,11 @@ def tile_reasoningmultiheadattention_pb_kernel(tc, h_attn, Wo, bo, out_0, out_1)
             multiply(t, 0)
         regroup(1, 0)
         quantize_y(3)
-        regroup(1, 1)
         for t in (2, 3):
             multiply(t, 0)
-        keep_bias(1)
-        for t in (0, 1):
-            finish_half(t, 0)
+        finish_half(0, 0)
+        regroup(1, 1)
+        finish_half(1, 0)
         cast_bytes(0, 0)
         for t in (4, 5, 6):
             turn(t)
@@ -262,6 +268,6 @@ def tile_reasoningmultiheadattention_pb_kernel(tc, h_attn, Wo, bo, out_0, out_1)
             if t + 2 < TILES:
                 multiply_tile(t + 2)
         for t in (6, 7):
-            for nh in range(2):
-                cast_bytes(t, nh)
+            cast_bytes(t, 0)
+            cast_bytes_on_vector(t, 1)
             store_bytes(t)

@@ -21,8 +21,8 @@ PASSES = 2
 HALF = 512
 TILES = 8
 ROWS = 32
-TURN_BANKS = 3
-SUM_BANKS = 5
+TURN_BANKS = 4
+SUM_BANKS = 4
 TURN_LEAD = 2
 
 
@@ -232,8 +232,10 @@ def tile_reasoningmultiheadattention_pb_kernel(tc, h_attn, Wo, bo, out_0, out_1)
         regroup(1, 1)
         finish_half(1, 0)
         cast_bytes(0, 0)
-        for t in (4, 5, 6):
+        for t in (4, 5):
             turn(t)
+        keep_tensor_busy(y_raw[1][:, 0, :])
+        turn(6)
         quantize_w(1, 1)
         for t in (2, 3):
             finish_half(t, 0)

from contextlib import ExitStack

import concourse.mybir as mybir
from concourse.masks import make_identity

FLOPS = 2 * 1024 * 1024 * 1024

F32 = mybir.dt.float32
BF16 = mybir.dt.bfloat16
U32 = mybir.dt.uint32
U8 = mybir.dt.uint8
FP8X4 = mybir.dt.float8_e4m3fn_x4
FP8 = mybir.dt.float8_e4m3fn
ADD = mybir.AluOpType.add
MULT = mybir.AluOpType.mult
COPY = mybir.ActivationFunctionType.Copy

P = 128
Y_SCALE = 400.0
PASSES = 2
HALF = 512
TILES = 8
ROWS = 32
TURN_BANKS = 4
SUM_BANKS = 4
TURN_LEAD = 2


def tile_reasoningmultiheadattention_pb_kernel(tc, h_attn, Wo, bo, out_0, out_1):
    nc = tc.nc
    with ExitStack() as ctx:
        keep = ctx.enter_context(tc.tile_pool(name="keep", bufs=1))
        turn_banks = ctx.enter_context(tc.psum_pool(name="turn_banks", bufs=TURN_BANKS))
        sum_banks = ctx.enter_context(tc.psum_pool(name="sum_banks", bufs=SUM_BANKS))
        ctx.enter_context(tc.manual_schedule())

        y_hbm = h_attn.rearrange("b (x j) h d -> (b x) j (h d)", j=8)
        w_hbm = Wo.rearrange("(g p t) n -> g p t n", g=PASSES, t=4)

        y_raw = [keep.tile([P, 8, 512], BF16, name="y_raw%d" % hh) for hh in range(2)]
        y_heads = [keep.tile([P, 8, 2, 128], F32, name="y_heads%d" % hh, align_bytes=64) for hh in range(2)]
        y_grouped = [keep.tile([P, PASSES, 128, 2], F32, name="y_grouped%d" % t, align_bytes=64) for t in range(TILES)]
        y_codes = [keep.tile([P, PASSES * 128], U32, name="y_codes%d" % t, align_bytes=64) for t in range(TILES)]
        y_scales = [keep.tile([P, PASSES * 128], U8, name="y_scales%d" % t, align_bytes=64) for t in range(TILES)]
        w_raw = {}
        w_grouped = {}
        for nh in range(2):
            for g in range(PASSES):
                w_raw[(nh, g)] = keep.tile([P, 4, HALF], BF16, name="w_raw%d%d" % (nh, g))
                w_grouped[(nh, g)] = keep.tile([P, HALF, 4], BF16, name="w_grouped%d%d" % (nh, g), align_bytes=64)
        w_codes = [keep.tile([P, 2 * HALF], U32, name="w_codes%d" % g, align_bytes=64) for g in range(PASSES)]
        w_scales = [keep.tile([P, 2 * HALF], U8, name="w_scales%d" % g, align_bytes=64) for g in range(PASSES)]
        res = [keep.tile([P, 2 * HALF], F32, name="res%d" % t) for t in range(TILES)]
        res_fp8 = [keep.tile([P, 2 * HALF], FP8, name="res_fp8_%d" % t) for t in range(TILES)]

        ident = keep.tile([P, P], F32, name="ident")
        perm = keep.tile([P, P], F32, name="perm")
        ones = keep.tile([P, P], BF16, name="ones")
        bias_row = keep.tile([P, 2 * HALF], BF16, name="bias_row")
        bias = keep.tile([P, 2 * HALF], BF16, name="bias")
        bank_of = {}

        def halfcols(nh):
            return slice(HALF * nh, HALF * nh + HALF)

        def load_y(hh, jh):
            tokens = slice(4 * jh, 4 * jh + 4)
            nc.sync.dma_start(out=y_raw[hh][:, tokens, :], in_=y_hbm[:, tokens, 512 * hh : 512 * hh + 512])

        def load_w(nh, g):
            nc.sync.dma_start(out=w_raw[(nh, g)][:], in_=w_hbm[g][:, :, halfcols(nh)])

        nc.vector.memset(bias_row[:], 0.0)
        for g in range(PASSES):
            load_w(0, g)
        nc.sync.dma_start(out=bias_row[0:1, :], in_=bo.rearrange("(o n) -> o n", o=1))
        for jh in range(2):
            load_y(0, jh)
        for g in range(PASSES):
            load_w(1, g)
        for jh in range(2):
            load_y(1, jh)

        nc.gpsimd.memset(ones[:], 1.0)
        make_identity(nc, ident[:])
        nc.vector.tensor_copy(
            out=perm[:].rearrange("p (g q b) -> p g q b", g=2, b=4),
            in_=ident[:].rearrange("p (b q g) -> p g q b", b=4, g=2),
        )

        def keep_tensor_busy(loaded):
            unread = turn_banks.tile([P, HALF], F32, name="unread", tag="turn")
            for repeat in range(2):
                nc.tensor.matmul(out=unread[:, 0:P], lhsT=ident[:], rhs=loaded.bitcast(F32)[:, 0:P], start=True, stop=True)

        def spread_bias(nh):
            if nh == 0:
                bank_of["bias"] = sum_banks.tile([P, 2 * HALF], BF16, name="sums")
            nc.tensor.matmul(
                out=bank_of["bias"][:, halfcols(nh)], lhsT=ones[:], rhs=bias_row[:, halfcols(nh)], start=True, stop=True
            )

        def keep_bias():
            nc.scalar.copy(out=bias[:], in_=bank_of["bias"][:])

        def regroup(hh, jh):
            words = y_raw[hh][:].rearrange("p j c -> p (j c)").bitcast(F32)
            src = words.rearrange("p (j h e u) -> p h u j e", j=8, h=8, u=2)
            dst = y_heads[hh][:].rearrange("p h u (j e) -> p h u j e", j=8)
            tokens = slice(4 * jh, 4 * jh + 4)
            nc.vector.tensor_copy(out=dst[:, :, :, tokens, :], in_=src[:, :, :, tokens, :])

        def turn(t):
            hh, pair = divmod(t, 4)
            bank = turn_banks.tile([P, 2, PASSES, 2, 64], F32, name="turned", tag="turn")
            bank_of[("turned", t)] = bank
            for hl in range(2):
                for u in range(2):
                    nc.tensor.transpose(out=bank[:, u, :, hl, :], in_=y_heads[hh][:, 2 * pair + hl, u, :], identity=perm[:])

        def unload(t):
            nc.scalar.copy(out=y_grouped[t][:], in_=bank_of[("turned", t)][:].rearrange("p u g hl x -> p g (hl x) u"))

        def quantize_y(t):
            nc.vector.quantize_mx(
                out=y_codes[t][:].bitcast(FP8X4),
                scales=y_scales[t][:],
                in_=y_grouped[t][:].rearrange("p g m u -> p (g m u)").bitcast(BF16),
            )

        def interleave_w(copy, nh, g):
            copy(
                out=w_grouped[(nh, g)][:].rearrange("p (c i) t -> p c t i", i=4),
                in_=w_raw[(nh, g)][:].rearrange("p t (c i) -> p c t i", i=4),
            )

        def quantize_w(nh, g):
            nc.vector.quantize_mx(
                out=w_codes[g][:, halfcols(nh)].bitcast(FP8X4),
                scales=w_scales[g][:, halfcols(nh)],
                in_=w_grouped[(nh, g)][:].rearrange("p c t -> p (c t)"),
            )

        def multiply(t, nh):
            sums = sum_banks.tile([P, HALF], F32, name="sums")
            bank_of[("sums", t, nh)] = sums
            for g in range(PASSES):
                of_pass = slice(128 * g, 128 * g + 128)
                nc.tensor.matmul_mx(
                    out=sums[:],
                    lhsT=y_codes[t][:, of_pass].bitcast(FP8X4),
                    lhsT_scale=y_scales[t][:, of_pass],
                    rhs=w_codes[g][:, halfcols(nh)].bitcast(FP8X4),
                    rhs_scale=w_scales[g][:, halfcols(nh)],
                    start=(g == 0),
                    stop=(g == PASSES - 1),
                )

        def add_bias(t, nh):
            nc.vector.tensor_tensor(out=res[t][:, halfcols(nh)], in0=bank_of[("sums", t, nh)][:], in1=bias[:, halfcols(nh)], op=ADD)

        def cast_bytes_on_vector(t, nh):
            nc.vector.tensor_scalar(
                out=res_fp8[t][:, halfcols(nh)], in0=res[t][:, halfcols(nh)], scalar1=Y_SCALE, scalar2=None, op0=MULT, saturate=False
            )

        def cast_bytes(t, nh):
            nc.scalar.activation(
                out=res_fp8[t][:, halfcols(nh)], in_=res[t][:, halfcols(nh)], func=COPY, scale=Y_SCALE, saturate=False
            )

        def store_floats(t, cols):
            rows = slice(ROWS * t, ROWS * t + ROWS)
            nc.sync.dma_start(out=out_0[:, rows, cols].rearrange("b r n -> r b n"), in_=res[t][:, cols])

        def store_bytes(t):
            rows = slice(ROWS * t, ROWS * t + ROWS)
            nc.sync.dma_start(out=out_1[:, rows, :].rearrange("b r n -> r b n"), in_=res_fp8[t][:].bitcast(U8))

        whole_rows = slice(0, 2 * HALF)

        def finish_half(t, nh):
            add_bias(t, nh)
            store_floats(t, halfcols(nh))

        def finish_whole(t):
            for nh in range(2):
                add_bias(t, nh)
            store_floats(t, whole_rows)

        def multiply_tile(t):
            for nh in range(2):
                multiply(t, nh)

        keep_tensor_busy(w_raw[(0, 0)][:, 0, :])
        interleave_w(nc.vector.tensor_copy, 0, 0)
        interleave_w(nc.scalar.copy, 0, 1)
        keep_tensor_busy(w_raw[(0, 1)][:, 0, :])
        for nh in range(2):
            spread_bias(nh)
        quantize_w(0, 0)
        keep_tensor_busy(y_raw[0][:, 0, :])
        regroup(0, 0)
        keep_tensor_busy(y_raw[0][:, 4, :])
        regroup(0, 1)
        quantize_w(0, 1)
        keep_bias()
        for t in (0, 1):
            turn(t)
        unload(0)
        turn(2)
        unload(1)
        keep_tensor_busy(y_raw[0][:, 4, :])
        turn(3)
        for t in (2, 3):
            unload(t)
        keep_tensor_busy(w_raw[(1, 0)][:, 0, :])

        interleave_w(nc.vector.tensor_copy, 1, 0)
        interleave_w(nc.scalar.copy, 1, 1)
        quantize_y(0)
        quantize_w(1, 0)
        quantize_y(1)
        quantize_y(2)
        for t in (0, 1):
            multiply(t, 0)
        regroup(1, 0)
        quantize_y(3)
        for t in (2, 3):
            multiply(t, 0)
        finish_half(0, 0)
        regroup(1, 1)
        finish_half(1, 0)
        cast_bytes(0, 0)
        for t in (4, 5):
            turn(t)
        keep_tensor_busy(y_raw[1][:, 0, :])
        turn(6)
        quantize_w(1, 1)
        for t in (2, 3):
            finish_half(t, 0)
        for t in range(4):
            multiply(t, 1)
        for t in (4, 5, 6):
            unload(t)
        turn(7)
        for t in (0, 1):
            finish_half(t, 1)
        cast_bytes(1, 0)
        cast_bytes(0, 1)
        store_bytes(0)
        quantize_y(4)
        finish_half(2, 1)
        cast_bytes(1, 1)
        store_bytes(1)
        unload(7)
        quantize_y(5)
        finish_half(3, 1)
        multiply_tile(4)
        quantize_y(6)
        multiply_tile(5)

        for t in range(4, 8):
            for nh in range(2):
                cast_bytes(t - 2, nh)
            store_bytes(t - 2)
            finish_whole(t)
            if t == 4:
                quantize_y(7)
            if t + 2 < TILES:
                multiply_tile(t + 2)
        for t in (6, 7):
            cast_bytes(t, 0)
            cast_bytes_on_vector(t, 1)
            store_bytes(t)
